import numpy as np
import ml_dtypes


def mxq(x, axis, fmt="e4m3"):
    dtype, down = {"e4m3": (ml_dtypes.float8_e4m3fn, 7), "e5m2": (ml_dtypes.float8_e5m2, 14)}[fmt]
    v = np.moveaxis(np.asarray(x, np.float32).astype(ml_dtypes.bfloat16).astype(np.float64), axis, -1)
    blocks = v.reshape(v.shape[:-1] + (-1, 32))
    amax = np.abs(blocks).max(-1, keepdims=True)
    byte = np.maximum(np.where(amax > 0, np.frexp(amax)[1] - 1 + 127, 0) - down, 1)
    scale = np.exp2(byte - 127.0)
    codes = (blocks / scale).astype(np.float32).astype(dtype).astype(np.float64)
    return np.moveaxis((codes * scale).reshape(v.shape), -1, axis)


WIDE = False


def mx_kscale(k):
    if not WIDE:
        return np.ones(k)
    levels = np.array([10, -10, 5, -5, 0])
    a = np.random.permutation(np.resize(levels, k // 512 * 4)).reshape(k // 512, 4)
    idx = np.arange(k)
    return np.exp2(a[idx // 512, idx % 128 // 32])


BF16 = ml_dtypes.bfloat16


def bf(x):
    return np.asarray(x, np.float32).astype(BF16)


def f64(x):
    return np.asarray(x).astype(np.float64)


B, F, DOF, N_CLS = 256, 256, 64, 1024
K = F * DOF


def setup_inputs():
    s = mx_kscale(K)
    c = s.max() / s.min()
    far = (s.reshape(F, 2, 32)[:, :, 0] == s.max()) & (c > 1.0)
    far[:, 1] &= ~far[:, 0]
    lo, hi = -3.0 / c, 3.0
    pos = 0.5 + np.random.standard_normal((B, F)) / 6.0
    pos = np.where(far[:, 1], 0.48 * np.minimum(pos, 1.0), pos)
    pos = np.where(far[:, 0], 1.0 - 0.48 * (1.0 - np.maximum(pos, 0.0)), pos)
    xv = f64(bf(lo + (hi - lo) * pos))
    xv[xv == hi] = 2.5
    xv[xv == lo] = -2.5
    wf = (np.where(far, c, 1.0)[:, :, None] * np.ones(32)).reshape(K)
    return {"x": bf(xv), "min_x": bf(np.array([lo])), "max_x": bf(np.array([hi])),
            "W": bf(np.random.standard_normal((N_CLS, K)) * 0.005 * wf), "dof": DOF}


def _lagrange_embed(x, min_x, max_x, dof):
    b_, f_ = x.shape
    T = dof - 1
    h = 1.0 / T
    xn = ((x.reshape(-1, 1) - min_x) / (max_x - min_x)).reshape(-1)
    t = np.arange(T, dtype=np.float64)
    s = xn[:, None] / h
    lam0 = s - t
    lam1 = (t + 1.0) - s
    n2t = ((lam0 >= 0.0) & (lam1 >= 0.0)).astype(np.float64)
    z = np.zeros((xn.shape[0], 1), dtype=np.float64)
    mask = np.concatenate([n2t, z], axis=1) + np.concatenate([z, n2t], axis=1)
    w0 = n2t * lam0
    w1 = n2t * lam1
    shape_vals = np.concatenate([w1, z], axis=1) + np.concatenate([z, w0], axis=1)
    basis = shape_vals / np.maximum(mask, 1.0)
    emb = basis * (max_x - min_x) + min_x
    return emb.reshape(b_, f_ * dof)


def reference(x, min_x, max_x, W, dof):
    emb = _lagrange_embed(f64(x), f64(min_x), f64(max_x), int(dof))
    return mxq(emb, 1, "e4m3") @ mxq(f64(W), 1, "e4m3").T

@@ -1,0 +1,268 @@
+from contextlib import ExitStack
+
+import concourse.mybir as mybir
+from concourse.masks import make_identity
+
+F32 = mybir.dt.float32
+BF16 = mybir.dt.bfloat16
+U32 = mybir.dt.uint32
+U8 = mybir.dt.uint8
+I32 = mybir.dt.int32
+FP8X4 = mybir.dt.float8_e4m3fn_x4
+ALU = mybir.AluOpType
+ACTF = mybir.ActivationFunctionType
+
+P = 128
+K_PASS = 512
+FLOPS = 2 * 256 * 1024 * 16384
+
+CHUNKS = [512, 512, 1024] + [2048] * 7
+WR_BUFS = 24
+
+
+def dve_exits(s):
+    return (0, 2) if s % 3 == 2 else (0,)
+
+
+def tile_lagrangenet_kernel(tc, x, min_x, max_x, W, dof, out):
+    nc = tc.nc
+    B, F = x.shape
+    N, K = W.shape
+    assert (B, F, N, K, dof) == (256, 256, 1024, 16384, 64)
+    n_pass = K // K_PASS
+    n_tiles = N // P
+    steps = float(dof - 1)
+
+    with ExitStack() as ctx:
+        ctx.enter_context(tc.manual_schedule())
+        const = ctx.enter_context(tc.tile_pool(name="const", bufs=1))
+        wrp = ctx.enter_context(tc.tile_pool(name="wrp", bufs=WR_BUFS))
+        gwp = ctx.enter_context(tc.tile_pool(name="gwp", bufs=3))
+        wcp = ctx.enter_context(tc.tile_pool(name="wcp", bufs=3))
+        emp = ctx.enter_context(tc.tile_pool(name="emp", bufs=2))
+        ecp = ctx.enter_context(tc.tile_pool(name="ecp", bufs=3))
+        resp = ctx.enter_context(tc.tile_pool(name="resp", bufs=4))
+        ps_acc = ctx.enter_context(tc.psum_pool(name="ps_acc", bufs=1))
+        ps_x = ctx.enter_context(tc.psum_pool(name="ps_x", bufs=1))
+        ps_t = ctx.enter_context(tc.psum_pool(name="ps_t", bufs=3))
+
+        x_sb = const.tile([P, 2, F], BF16, name="x_sb")
+        nc.sync.dma_start(out=x_sb[:], in_=x.rearrange("(t p) f -> p t f", p=P))
+        mn_bf = const.tile([P, 1], BF16, name="mn_bf")
+        mx_bf = const.tile([P, 1], BF16, name="mx_bf")
+        nc.scalar.dma_start(out=mn_bf[:], in_=min_x.partition_broadcast(P))
+        nc.scalar.dma_start(out=mx_bf[:], in_=max_x.partition_broadcast(P))
+
+        chunk_start = []
+        k0 = 0
+        for kc in CHUNKS:
+            chunk_start.append(k0)
+            k0 += kc
+        assert k0 == K
+        pass_chunk = []
+        for c, kc in enumerate(CHUNKS):
+            for gl in range(kc // K_PASS):
+                pass_chunk.append((c, gl))
+        wr_tiles = {}
+
+        def load_chunk(c):
+            kc = CHUNKS[c]
+            for j in range(n_tiles):
+                wr = wrp.tile([P, kc], BF16, name="wr", tag="wr")
+                nc.sync.dma_start(
+                    out=wr[:], in_=W[j * P : (j + 1) * P, chunk_start[c] : chunk_start[c] + kc]
+                )
+                wr_tiles[(c, j)] = wr
+
+        resident = WR_BUFS // n_tiles
+        for c in range(resident):
+            load_chunk(c)
+
+        ident = const.tile([P, P], F32, name="ident")
+        make_identity(nc, ident[:])
+        vi = const.tile([P, 2], I32, name="vi")
+        nc.gpsimd.iota(vi[:], pattern=[[1, 2]], base=0, channel_multiplier=2)
+        big = const.tile([P, P, 32], BF16, name="big")
+        for lo, hi in ((0, 32), (32, P)):
+            nc.gpsimd.tensor_scalar(
+                out=big[:, lo:hi, :],
+                in0=ident[:, lo:hi].unsqueeze(2).to_broadcast([P, hi - lo, 32]),
+                scalar1=1.0,
+                scalar2=0.0,
+                op0=ALU.mult,
+                op1=ALU.add,
+            )
+        bigf = big[:].rearrange("p f r -> p (f r)")
+
+        warm = const.tile([P, 1], F32, name="warm")
+        nc.scalar.activation(out=warm[:], in_=ident[:, 0:1], func=ACTF.Abs)
+
+        sc = const.tile([P, 8], F32, name="sc")
+        mn = sc[:, 0:1]
+        mx = sc[:, 1:2]
+        nrg = sc[:, 2:3]
+        nmn = sc[:, 3:4]
+        c63 = sc[:, 4:5]
+        k2 = sc[:, 5:6]
+        nc.vector.tensor_copy(out=mn, in_=mn_bf[:])
+        nc.vector.tensor_copy(out=mx, in_=mx_bf[:])
+        nc.vector.tensor_sub(out=nrg, in0=mn, in1=mx)
+        nc.vector.tensor_scalar(out=nmn, in0=mn, scalar1=-1.0, scalar2=None, op0=ALU.mult)
+        nc.vector.tensor_scalar(out=c63, in0=mn, scalar1=-steps, scalar2=None, op0=ALU.mult)
+        nc.vector.tensor_scalar(out=k2, in0=nrg, scalar1=-2.0, scalar2=None, op0=ALU.mult)
+
+        vm = const.tile([P, 2], I32, name="vm")
+        nc.vector.tensor_single_scalar(out=vm[:], in_=vi[:], scalar=dof - 1, op=ALU.bitwise_and)
+        vf = const.tile([P, 2], F32, name="vf")
+        nc.vector.tensor_copy(out=vf[:], in_=vm[:])
+        bias = const.tile([P, 2], F32, name="bias")
+        nc.vector.tensor_scalar(out=bias[:], in0=vf[:], scalar1=nrg, scalar2=c63, op0=ALU.mult, op1=ALU.add)
+
+        xf = const.tile([P, 2, F], F32, name="xf")
+        gt = const.tile([P, 2, F], F32, name="gt")
+        lt = const.tile([P, 2, F], F32, name="lt")
+        nc.vector.tensor_copy(out=xf[:], in_=x_sb[:])
+        nc.vector.tensor_scalar(out=gt[:], in0=xf[:], scalar1=mx, scalar2=k2, op0=ALU.is_gt, op1=ALU.mult)
+        nc.vector.tensor_scalar(out=lt[:], in0=xf[:], scalar1=mn, scalar2=k2, op0=ALU.is_lt, op1=ALU.mult)
+        nc.vector.tensor_sub(out=gt[:], in0=gt[:], in1=lt[:])
+        nc.vector.tensor_add(out=xf[:], in0=xf[:], in1=gt[:])
+
+        xtp = ps_x.tile([P, 2, B], F32, name="xtp", tag="xb")
+        for ft in range(2):
+            for t in range(2):
+                nc.tensor.transpose(
+                    xtp[:, ft, t * P : (t + 1) * P], xf[:, t, ft * P : (ft + 1) * P], ident[:]
+                )
+        xT = const.tile([P, 2, B], BF16, name="xT")
+        nc.vector.tensor_copy(out=xT[:], in_=xtp[:])
+
+        acc = {}
+        for bt in range(2):
+            for h in range(2):
+                acc[(bt, h)] = ps_acc.tile([P, 512], F32, name="acc%d%d" % (bt, h))
+
+        xb_t = {}
+        a_t = {}
+        ge_t = {}
+        ec_t = {}
+        gw_t = {}
+        wc_t = {}
+
+        def tx(g):
+            xb = ps_x.tile([P, 2, B], F32, name="xb", tag="xb")
+            for u in range(2):
+                m = 2 * (g % 16) + u
+                nc.tensor.matmul(
+                    xb[:, u, :],
+                    lhsT=bigf[:, m * P : (m + 1) * P],
+                    rhs=xT[:, g // 16, :],
+                    start=True,
+                    stop=True,
+                )
+            xb_t[g] = xb
+
+        def a1(g):
+            a = emp.tile([P, 2, 2 * B], F32, name="a", tag="a")
+            for e in range(2):
+                nc.scalar.activation(
+                    out=a[:, e, :].rearrange("p (b u) -> p b u", u=2),
+                    in_=xb_t[g][:].rearrange("p u b -> p b u"),
+                    func=ACTF.Abs,
+                    bias=bias[:, e : e + 1],
+                    scale=steps,
+                )
+            a_t[g] = a
+
+        def a2(g):
+            ge = emp.tile([P, 4 * B], BF16, name="ge", tag="ge", align_bytes=64)
+            nc.vector.tensor_scalar(
+                out=ge[:].rearrange("p (c e) -> p c e", e=2),
+                in0=a_t[g][:].rearrange("p e c -> p c e"),
+                scalar1=mx,
+                scalar2=nmn,
+                op0=ALU.subtract,
+                op1=ALU.min,
+            )
+            ge_t[g] = ge
+
+        def qe(g):
+            ec = ecp.tile([P, B], U32, name="ec", tag="ec", align_bytes=64)
+            es = ecp.tile([P, B], U8, name="es", tag="es", align_bytes=64)
+            nc.vector.quantize_mx(out=ec[:].bitcast(FP8X4), scales=es[:], in_=ge_t[g][:])
+            ec_t[g] = (ec, es)
+
+        def t_run(g):
+            c, gl = pass_chunk[g]
+            gw = gwp.tile([P, 4 * N], BF16, name="gw", tag="gw", align_bytes=64)
+            gw32 = gw[:].bitcast(F32)
+            on_dve = dve_exits(g)
+            for r in range(4):
+                tw = ps_t.tile([P, 4, P], F32, name="tw", tag="tw")
+                for jj in range(2):
+                    w32 = wr_tiles[(c, 2 * r + jj)][:].bitcast(F32)
+                    for u in range(2):
+                        w0 = 256 * gl + P * u
+                        nc.tensor.transpose(tw[:, 2 * jj + u, :], w32[:, w0 : w0 + P], ident[:])
+                dst = gw32[:, 512 * r : 512 * (r + 1)].rearrange("p (j n u) -> p j n u", j=2, u=2)
+                src = tw[:].rearrange("p (j u) n -> p j n u", u=2)
+                if r in on_dve:
+                    nc.vector.tensor_copy(out=dst, in_=src)
+                else:
+                    nc.scalar.copy(out=dst, in_=src)
+            gw_t[g] = gw
+
+        def qw(g):
+            wc = wcp.tile([P, N], U32, name="wc", tag="wc", align_bytes=64)
+            ws = wcp.tile([P, N], U8, name="ws", tag="ws", align_bytes=64)
+            nc.vector.quantize_mx(out=wc[:].bitcast(FP8X4), scales=ws[:], in_=gw_t[g][:])
+            wc_t[g] = (wc, ws)
+
+        def mm(g):
+            ec, es = ec_t[g]
+            wc, ws = wc_t[g]
+            for h in range(2):
+                for bt in range(2):
+                    nc.tensor.matmul_mx(
+                        out=acc[(bt, h)][:],
+                        lhsT=ec[:, bt * P : (bt + 1) * P].bitcast(FP8X4),
+                        lhsT_scale=es[:, bt * P : (bt + 1) * P],
+                        rhs=wc[:, h * 512 : (h + 1) * 512].bitcast(FP8X4),
+                        rhs_scale=ws[:, h * 512 : (h + 1) * 512],
+                        start=(g == 0),
+                        stop=(g == n_pass - 1),
+                    )
+
+        tx(0)
+        for s in range(n_pass + 2):
+            if 0 <= s - 1 < n_pass:
+                qe(s - 1)
+            if s < n_pass:
+                a1(s)
+                t_run(s)
+            if 0 <= s - 1 < n_pass:
+                qw(s - 1)
+            if s < n_pass:
+                a2(s)
+            if 0 <= s - 2:
+                mm(s - 2)
+            if s + 1 < n_pass:
+                tx(s + 1)
+            if s < n_pass:
+                c, gl = pass_chunk[s]
+                if gl == CHUNKS[c] // K_PASS - 1 and c + resident < len(CHUNKS):
+                    load_chunk(c + resident)
+
+        i = 0
+        for h in range(2):
+            for bt in range(2):
+                res = resp.tile([P, 512], F32, name="res", tag="res")
+                if i % 2 == 0:
+                    nc.scalar.mul(out=res[:], in_=acc[(bt, h)][:], mul=-1.0)
+                else:
+                    nc.vector.tensor_scalar(
+                        out=res[:], in0=acc[(bt, h)][:], scalar1=-1.0, scalar2=None, op0=ALU.mult
+                    )
+                nc.sync.dma_start(
+                    out=out[bt * P : (bt + 1) * P, h * 512 : (h + 1) * 512], in_=res[:]
+                )
+                i += 1

@@ -16,12 +16,16 @@ P = 128
 K_PASS = 512
 FLOPS = 2 * 256 * 1024 * 16384
 
-CHUNKS = [512, 512, 1024] + [2048] * 7
+CHUNKS = [1024] * 6 + [2048] * 5
 WR_BUFS = 24
 
 
-def dve_exits(s):
-    return (0, 2) if s % 3 == 2 else (0,)
+def dve_units(s):
+    if s == 0:
+        return (0, 2)
+    if s == 1:
+        return (0, 1)
+    return (0,)
 
 
 def tile_lagrangenet_kernel(tc, x, min_x, max_x, W, dof, out):
@@ -37,14 +41,13 @@ def tile_lagrangenet_kernel(tc, x, min_x, max_x, W, dof, out):
         ctx.enter_context(tc.manual_schedule())
         const = ctx.enter_context(tc.tile_pool(name="const", bufs=1))
         wrp = ctx.enter_context(tc.tile_pool(name="wrp", bufs=WR_BUFS))
-        gwp = ctx.enter_context(tc.tile_pool(name="gwp", bufs=3))
-        wcp = ctx.enter_context(tc.tile_pool(name="wcp", bufs=3))
-        emp = ctx.enter_context(tc.tile_pool(name="emp", bufs=2))
-        ecp = ctx.enter_context(tc.tile_pool(name="ecp", bufs=3))
+        gwp = ctx.enter_context(tc.tile_pool(name="gwp", bufs=6))
+        wcp = ctx.enter_context(tc.tile_pool(name="wcp", bufs=6))
+        ap_ = ctx.enter_context(tc.tile_pool(name="ap", bufs=2))
+        gep = ctx.enter_context(tc.tile_pool(name="gep", bufs=3))
+        ecp = ctx.enter_context(tc.tile_pool(name="ecp", bufs=5))
         resp = ctx.enter_context(tc.tile_pool(name="resp", bufs=4))
-        ps_acc = ctx.enter_context(tc.psum_pool(name="ps_acc", bufs=1))
-        ps_x = ctx.enter_context(tc.psum_pool(name="ps_x", bufs=1))
-        ps_t = ctx.enter_context(tc.psum_pool(name="ps_t", bufs=3))
+        psum = ctx.enter_context(tc.psum_pool(name="psum", bufs=1))
 
         x_sb = const.tile([P, 2, F], BF16, name="x_sb")
         nc.sync.dma_start(out=x_sb[:], in_=x.rearrange("(t p) f -> p t f", p=P))
@@ -53,30 +56,39 @@ def tile_lagrangenet_kernel(tc, x, min_x, max_x, W, dof, out):
         nc.scalar.dma_start(out=mn_bf[:], in_=min_x.partition_broadcast(P))
         nc.scalar.dma_start(out=mx_bf[:], in_=max_x.partition_broadcast(P))
 
+        pass_chunk = []
+        load_order = []
         chunk_start = []
         k0 = 0
-        for kc in CHUNKS:
+        for c, kc in enumerate(CHUNKS):
             chunk_start.append(k0)
             k0 += kc
-        assert k0 == K
-        pass_chunk = []
-        for c, kc in enumerate(CHUNKS):
             for gl in range(kc // K_PASS):
                 pass_chunk.append((c, gl))
-        wr_tiles = {}
-
-        def load_chunk(c):
-            kc = CHUNKS[c]
             for j in range(n_tiles):
+                load_order.append((c, j))
+        assert k0 == K
+        wr_tiles = {}
+        wr_reads = {}
+        loaded = [0]
+
+        def try_load():
+            while loaded[0] < len(load_order):
+                n = loaded[0]
+                if n >= WR_BUFS:
+                    old = load_order[n - WR_BUFS]
+                    if wr_reads.get(old, 0) < CHUNKS[old[0]] // K_PASS:
+                        return
+                c, j = load_order[n]
+                kc = CHUNKS[c]
                 wr = wrp.tile([P, kc], BF16, name="wr", tag="wr")
                 nc.sync.dma_start(
                     out=wr[:], in_=W[j * P : (j + 1) * P, chunk_start[c] : chunk_start[c] + kc]
                 )
                 wr_tiles[(c, j)] = wr
+                loaded[0] = n + 1
 
-        resident = WR_BUFS // n_tiles
-        for c in range(resident):
-            load_chunk(c)
+        try_load()
 
         ident = const.tile([P, P], F32, name="ident")
         make_identity(nc, ident[:])
@@ -94,8 +106,19 @@ def tile_lagrangenet_kernel(tc, x, min_x, max_x, W, dof, out):
             )
         bigf = big[:].rearrange("p f r -> p (f r)")
 
-        warm = const.tile([P, 1], F32, name="warm")
-        nc.scalar.activation(out=warm[:], in_=ident[:, 0:1], func=ACTF.Abs)
+        warm_in = const.tile([P, 1], F32, name="warm_in")
+        warm_out = const.tile([P, 1], F32, name="warm_out")
+        nc.vector.memset(warm_in[:], 0.0)
+        nc.scalar.activation(out=warm_out[:], in_=warm_in[:], func=ACTF.Abs)
+        xf = const.tile([P, 2, F], F32, name="xf")
+        nc.scalar.copy(out=xf[:], in_=x_sb[:])
+
+        xtp = psum.tile([P, 2, B], F32, name="xtp", tag="acc11")
+        for ft in range(2):
+            for t in range(2):
+                nc.tensor.transpose(
+                    xtp[:, ft, t * P : (t + 1) * P], xf[:, t, ft * P : (ft + 1) * P], ident[:]
+                )
 
         sc = const.tile([P, 8], F32, name="sc")
         mn = sc[:, 0:1]
@@ -107,10 +130,9 @@ def tile_lagrangenet_kernel(tc, x, min_x, max_x, W, dof, out):
         nc.vector.tensor_copy(out=mn, in_=mn_bf[:])
         nc.vector.tensor_copy(out=mx, in_=mx_bf[:])
         nc.vector.tensor_sub(out=nrg, in0=mn, in1=mx)
+        nc.vector.tensor_scalar(out=k2, in0=nrg, scalar1=-2.0, scalar2=None, op0=ALU.mult)
         nc.vector.tensor_scalar(out=nmn, in0=mn, scalar1=-1.0, scalar2=None, op0=ALU.mult)
         nc.vector.tensor_scalar(out=c63, in0=mn, scalar1=-steps, scalar2=None, op0=ALU.mult)
-        nc.vector.tensor_scalar(out=k2, in0=nrg, scalar1=-2.0, scalar2=None, op0=ALU.mult)
-
         vm = const.tile([P, 2], I32, name="vm")
         nc.vector.tensor_single_scalar(out=vm[:], in_=vi[:], scalar=dof - 1, op=ALU.bitwise_and)
         vf = const.tile([P, 2], F32, name="vf")
@@ -118,29 +140,33 @@ def tile_lagrangenet_kernel(tc, x, min_x, max_x, W, dof, out):
         bias = const.tile([P, 2], F32, name="bias")
         nc.vector.tensor_scalar(out=bias[:], in0=vf[:], scalar1=nrg, scalar2=c63, op0=ALU.mult, op1=ALU.add)
 
-        xf = const.tile([P, 2, F], F32, name="xf")
-        gt = const.tile([P, 2, F], F32, name="gt")
-        lt = const.tile([P, 2, F], F32, name="lt")
-        nc.vector.tensor_copy(out=xf[:], in_=x_sb[:])
-        nc.vector.tensor_scalar(out=gt[:], in0=xf[:], scalar1=mx, scalar2=k2, op0=ALU.is_gt, op1=ALU.mult)
-        nc.vector.tensor_scalar(out=lt[:], in0=xf[:], scalar1=mn, scalar2=k2, op0=ALU.is_lt, op1=ALU.mult)
-        nc.vector.tensor_sub(out=gt[:], in0=gt[:], in1=lt[:])
-        nc.vector.tensor_add(out=xf[:], in0=xf[:], in1=gt[:])
-
-        xtp = ps_x.tile([P, 2, B], F32, name="xtp", tag="xb")
-        for ft in range(2):
-            for t in range(2):
-                nc.tensor.transpose(
-                    xtp[:, ft, t * P : (t + 1) * P], xf[:, t, ft * P : (ft + 1) * P], ident[:]
-                )
         xT = const.tile([P, 2, B], BF16, name="xT")
-        nc.vector.tensor_copy(out=xT[:], in_=xtp[:])
+        below = const.tile([P, 2, B], F32, name="below")
+        side = const.tile([P, 2, B], F32, name="side")
+
+        def push_out(ft):
+            nc.vector.tensor_scalar(
+                out=below[:, ft, :], in0=xtp[:, ft, :], scalar1=mn, scalar2=None, op0=ALU.is_lt
+            )
+            nc.vector.scalar_tensor_tensor(
+                out=side[:, ft, :], in0=xtp[:, ft, :], scalar=mx, in1=below[:, ft, :],
+                op0=ALU.is_gt, op1=ALU.subtract,
+            )
+            nc.vector.scalar_tensor_tensor(
+                out=xT[:, ft, :], in0=side[:, ft, :], scalar=k2, in1=xtp[:, ft, :],
+                op0=ALU.mult, op1=ALU.add,
+            )
+
+        push_out(0)
+
+        bank_use = [0]
+
+        def next_bank():
+            tag = "rot%d" % (bank_use[0] % 4)
+            bank_use[0] += 1
+            return tag
 
         acc = {}
-        for bt in range(2):
-            for h in range(2):
-                acc[(bt, h)] = ps_acc.tile([P, 512], F32, name="acc%d%d" % (bt, h))
-
         xb_t = {}
         a_t = {}
         ge_t = {}
@@ -148,8 +174,8 @@ def tile_lagrangenet_kernel(tc, x, min_x, max_x, W, dof, out):
         gw_t = {}
         wc_t = {}
 
-        def tx(g):
-            xb = ps_x.tile([P, 2, B], F32, name="xb", tag="xb")
+        def tx(g, tag):
+            xb = psum.tile([P, 2, B], F32, name="xb", tag=tag)
             for u in range(2):
                 m = 2 * (g % 16) + u
                 nc.tensor.matmul(
@@ -162,7 +188,7 @@ def tile_lagrangenet_kernel(tc, x, min_x, max_x, W, dof, out):
             xb_t[g] = xb
 
         def a1(g):
-            a = emp.tile([P, 2, 2 * B], F32, name="a", tag="a")
+            a = ap_.tile([P, 2, 2 * B], F32, name="a", tag="a")
             for e in range(2):
                 nc.scalar.activation(
                     out=a[:, e, :].rearrange("p (b u) -> p b u", u=2),
@@ -174,7 +200,7 @@ def tile_lagrangenet_kernel(tc, x, min_x, max_x, W, dof, out):
             a_t[g] = a
 
         def a2(g):
-            ge = emp.tile([P, 4 * B], BF16, name="ge", tag="ge", align_bytes=64)
+            ge = gep.tile([P, 4 * B], BF16, name="ge", tag="ge", align_bytes=64)
             nc.vector.tensor_scalar(
                 out=ge[:].rearrange("p (c e) -> p c e", e=2),
                 in0=a_t[g][:].rearrange("p e c -> p c e"),
@@ -191,72 +217,57 @@ def tile_lagrangenet_kernel(tc, x, min_x, max_x, W, dof, out):
             nc.vector.quantize_mx(out=ec[:].bitcast(FP8X4), scales=es[:], in_=ge_t[g][:])
             ec_t[g] = (ec, es)
 
-        def t_run(g):
+        def unit(g, r, on_dve):
             c, gl = pass_chunk[g]
-            gw = gwp.tile([P, 4 * N], BF16, name="gw", tag="gw", align_bytes=64)
-            gw32 = gw[:].bitcast(F32)
-            on_dve = dve_exits(g)
-            for r in range(4):
-                tw = ps_t.tile([P, 4, P], F32, name="tw", tag="tw")
-                for jj in range(2):
-                    w32 = wr_tiles[(c, 2 * r + jj)][:].bitcast(F32)
-                    for u in range(2):
-                        w0 = 256 * gl + P * u
-                        nc.tensor.transpose(tw[:, 2 * jj + u, :], w32[:, w0 : w0 + P], ident[:])
-                dst = gw32[:, 512 * r : 512 * (r + 1)].rearrange("p (j n u) -> p j n u", j=2, u=2)
-                src = tw[:].rearrange("p (j u) n -> p j n u", u=2)
-                if r in on_dve:
-                    nc.vector.tensor_copy(out=dst, in_=src)
-                else:
-                    nc.scalar.copy(out=dst, in_=src)
-            gw_t[g] = gw
+            h = r // 2
+            if (g, h) not in gw_t:
+                gw_t[(g, h)] = gwp.tile([P, 2 * N], BF16, name="gw", tag="gw", align_bytes=64)
+            gw32 = gw_t[(g, h)][:].bitcast(F32)
+            tw = psum.tile([P, 4, P], F32, name="tw", tag=next_bank())
+            for jj in range(2):
+                j = 2 * r + jj
+                w32 = wr_tiles[(c, j)][:].bitcast(F32)
+                for u in range(2):
+                    w0 = 256 * gl + P * u
+                    nc.tensor.transpose(tw[:, 2 * jj + u, :], w32[:, w0 : w0 + P], ident[:])
+                wr_reads[(c, j)] = wr_reads.get((c, j), 0) + 1
+            part = r % 2
+            dst = gw32[:, 512 * part : 512 * (part + 1)].rearrange("p (j n u) -> p j n u", j=2, u=2)
+            src = tw[:].rearrange("p (j u) n -> p j n u", u=2)
+            if on_dve:
+                nc.vector.tensor_copy(out=dst, in_=src)
+            else:
+                nc.scalar.copy(out=dst, in_=src)
+            try_load()
 
-        def qw(g):
-            wc = wcp.tile([P, N], U32, name="wc", tag="wc", align_bytes=64)
-            ws = wcp.tile([P, N], U8, name="ws", tag="ws", align_bytes=64)
-            nc.vector.quantize_mx(out=wc[:].bitcast(FP8X4), scales=ws[:], in_=gw_t[g][:])
-            wc_t[g] = (wc, ws)
+        def qw(g, h):
+            wc = wcp.tile([P, 512], U32, name="wc", tag="wc", align_bytes=64)
+            ws = wcp.tile([P, 512], U8, name="ws", tag="ws", align_bytes=64)
+            nc.vector.quantize_mx(out=wc[:].bitcast(FP8X4), scales=ws[:], in_=gw_t[(g, h)][:])
+            wc_t[(g, h)] = (wc, ws)
 
-        def mm(g):
+        def mm(g, h):
             ec, es = ec_t[g]
-            wc, ws = wc_t[g]
-            for h in range(2):
-                for bt in range(2):
-                    nc.tensor.matmul_mx(
-                        out=acc[(bt, h)][:],
-                        lhsT=ec[:, bt * P : (bt + 1) * P].bitcast(FP8X4),
-                        lhsT_scale=es[:, bt * P : (bt + 1) * P],
-                        rhs=wc[:, h * 512 : (h + 1) * 512].bitcast(FP8X4),
-                        rhs_scale=ws[:, h * 512 : (h + 1) * 512],
-                        start=(g == 0),
-                        stop=(g == n_pass - 1),
+            wc, ws = wc_t[(g, h)]
+            for bt in range(2):
+                if (bt, h) not in acc:
+                    acc[(bt, h)] = psum.tile(
+                        [P, 512], F32, name="acc%d%d" % (bt, h), tag="acc%d%d" % (bt, h)
                     )
+                nc.tensor.matmul_mx(
+                    out=acc[(bt, h)][:],
+                    lhsT=ec[:, bt * P : (bt + 1) * P].bitcast(FP8X4),
+                    lhsT_scale=es[:, bt * P : (bt + 1) * P],
+                    rhs=wc[:].bitcast(FP8X4),
+                    rhs_scale=ws[:],
+                    start=(g == 0),
+                    stop=(g == n_pass - 1),
+                )
 
-        tx(0)
-        for s in range(n_pass + 2):
-            if 0 <= s - 1 < n_pass:
-                qe(s - 1)
-            if s < n_pass:
-                a1(s)
-                t_run(s)
-            if 0 <= s - 1 < n_pass:
-                qw(s - 1)
-            if s < n_pass:
-                a2(s)
-            if 0 <= s - 2:
-                mm(s - 2)
-            if s + 1 < n_pass:
-                tx(s + 1)
-            if s < n_pass:
-                c, gl = pass_chunk[s]
-                if gl == CHUNKS[c] // K_PASS - 1 and c + resident < len(CHUNKS):
-                    load_chunk(c + resident)
-
-        i = 0
-        for h in range(2):
+        def finish(h):
             for bt in range(2):
                 res = resp.tile([P, 512], F32, name="res", tag="res")
-                if i % 2 == 0:
+                if bt == 0:
                     nc.scalar.mul(out=res[:], in_=acc[(bt, h)][:], mul=-1.0)
                 else:
                     nc.vector.tensor_scalar(
@@ -265,4 +276,41 @@ def tile_lagrangenet_kernel(tc, x, min_x, max_x, W, dof, out):
                 nc.sync.dma_start(
                     out=out[bt * P : (bt + 1) * P, h * 512 : (h + 1) * 512], in_=res[:]
                 )
-                i += 1
+
+        def items(s):
+            return ((2 * (s // 2), s % 2), (2 * (s // 2) + 1, s % 2))
+
+        for s in range(n_pass + 2):
+            last = s == n_pass - 1
+            if 1 <= s <= n_pass and not s == n_pass:
+                qe(s - 1)
+            if s < n_pass:
+                on_dve = dve_units(s)
+                (ga, h), (gb, hb) = items(s)
+                order = ((ga, 2 * h), (gb, 2 * h), (ga, 2 * h + 1), (gb, 2 * h + 1))
+                for i, (g, r) in enumerate(order):
+                    unit(g, r, i in on_dve)
+                if s == 0:
+                    tx(0, "acc10")
+                    tx(1, "acc01")
+                    a1(0)
+                elif s + 1 < n_pass:
+                    tx(s + 1, next_bank())
+            if last:
+                a2(s)
+            if 1 <= s <= n_pass:
+                for g, h in items(s - 1):
+                    qw(g, h)
+            if last:
+                qe(s)
+            if s < n_pass and not last:
+                a2(s)
+            if s == 1:
+                push_out(1)
+            if s + 1 < n_pass:
+                a1(s + 1)
+            if s >= 2:
+                for g, h in items(s - 2):
+                    mm(g, h)
+                    if g == n_pass - 1:
+                        finish(h)

@@ -25,7 +25,9 @@ def dve_units(s):
         return (0, 2)
     if s == 1:
         return (0, 1)
-    return (0,)
+    if s == 31:
+        return ()
+    return (3,)
 
 
 def tile_lagrangenet_kernel(tc, x, min_x, max_x, W, dof, out):
@@ -217,7 +219,13 @@ def tile_lagrangenet_kernel(tc, x, min_x, max_x, W, dof, out):
             nc.vector.quantize_mx(out=ec[:].bitcast(FP8X4), scales=es[:], in_=ge_t[g][:])
             ec_t[g] = (ec, es)
 
-        def unit(g, r, on_dve):
+        def leave(dst, src, on_dve):
+            if on_dve:
+                nc.vector.tensor_copy(out=dst, in_=src)
+            else:
+                nc.scalar.copy(out=dst, in_=src)
+
+        def unit(g, r):
             c, gl = pass_chunk[g]
             h = r // 2
             if (g, h) not in gw_t:
@@ -234,11 +242,8 @@ def tile_lagrangenet_kernel(tc, x, min_x, max_x, W, dof, out):
             part = r % 2
             dst = gw32[:, 512 * part : 512 * (part + 1)].rearrange("p (j n u) -> p j n u", j=2, u=2)
             src = tw[:].rearrange("p (j u) n -> p j n u", u=2)
-            if on_dve:
-                nc.vector.tensor_copy(out=dst, in_=src)
-            else:
-                nc.scalar.copy(out=dst, in_=src)
             try_load()
+            return dst, src
 
         def qw(g, h):
             wc = wcp.tile([P, 512], U32, name="wc", tag="wc", align_bytes=64)
@@ -282,6 +287,7 @@ def tile_lagrangenet_kernel(tc, x, min_x, max_x, W, dof, out):
 
         for s in range(n_pass + 2):
             last = s == n_pass - 1
+            late = []
             if 1 <= s <= n_pass and not s == n_pass:
                 qe(s - 1)
             if s < n_pass:
@@ -289,7 +295,11 @@ def tile_lagrangenet_kernel(tc, x, min_x, max_x, W, dof, out):
                 (ga, h), (gb, hb) = items(s)
                 order = ((ga, 2 * h), (gb, 2 * h), (ga, 2 * h + 1), (gb, 2 * h + 1))
                 for i, (g, r) in enumerate(order):
-                    unit(g, r, i in on_dve)
+                    dst, src = unit(g, r)
+                    if s >= 2 and i in on_dve:
+                        late.append((dst, src))
+                    else:
+                        leave(dst, src, i in on_dve)
                 if s == 0:
                     tx(0, "acc10")
                     tx(1, "acc01")
@@ -305,6 +315,8 @@ def tile_lagrangenet_kernel(tc, x, min_x, max_x, W, dof, out):
                 qe(s)
             if s < n_pass and not last:
                 a2(s)
+            for dst, src in late:
+                leave(dst, src, True)
             if s == 1:
                 push_out(1)
             if s + 1 < n_pass:

@@ -43,8 +43,8 @@ def tile_lagrangenet_kernel(tc, x, min_x, max_x, W, dof, out):
         ctx.enter_context(tc.manual_schedule())
         const = ctx.enter_context(tc.tile_pool(name="const", bufs=1))
         wrp = ctx.enter_context(tc.tile_pool(name="wrp", bufs=WR_BUFS))
-        gwp = ctx.enter_context(tc.tile_pool(name="gwp", bufs=6))
-        wcp = ctx.enter_context(tc.tile_pool(name="wcp", bufs=6))
+        gwp = ctx.enter_context(tc.tile_pool(name="gwp", bufs=3))
+        wcp = ctx.enter_context(tc.tile_pool(name="wcp", bufs=3))
         ap_ = ctx.enter_context(tc.tile_pool(name="ap", bufs=2))
         gep = ctx.enter_context(tc.tile_pool(name="gep", bufs=3))
         ecp = ctx.enter_context(tc.tile_pool(name="ecp", bufs=5))
@@ -228,9 +228,10 @@ def tile_lagrangenet_kernel(tc, x, min_x, max_x, W, dof, out):
         def unit(g, r):
             c, gl = pass_chunk[g]
             h = r // 2
-            if (g, h) not in gw_t:
-                gw_t[(g, h)] = gwp.tile([P, 2 * N], BF16, name="gw", tag="gw", align_bytes=64)
-            gw32 = gw_t[(g, h)][:].bitcast(F32)
+            key = (g // 2, h)
+            if key not in gw_t:
+                gw_t[key] = gwp.tile([P, 4 * N], BF16, name="gw", tag="gw", align_bytes=64)
+            gw32 = gw_t[key][:].bitcast(F32)[:, (g % 2) * N : (g % 2 + 1) * N]
             tw = psum.tile([P, 4, P], F32, name="tw", tag=next_bank())
             for jj in range(2):
                 j = 2 * r + jj
@@ -245,15 +246,23 @@ def tile_lagrangenet_kernel(tc, x, min_x, max_x, W, dof, out):
             try_load()
             return dst, src
 
-        def qw(g, h):
-            wc = wcp.tile([P, 512], U32, name="wc", tag="wc", align_bytes=64)
-            ws = wcp.tile([P, 512], U8, name="ws", tag="ws", align_bytes=64)
-            nc.vector.quantize_mx(out=wc[:].bitcast(FP8X4), scales=ws[:], in_=gw_t[(g, h)][:])
-            wc_t[(g, h)] = (wc, ws)
+        def qw(key):
+            wc = wcp.tile([P, N], U32, name="wc", tag="wc", align_bytes=64)
+            ws = wcp.tile([P, N], U8, name="ws", tag="ws", align_bytes=64)
+            pieces = 2 if key == (n_pass // 2 - 1, 1) else 1
+            w = N // pieces
+            for i in range(pieces):
+                nc.vector.quantize_mx(
+                    out=wc[:, i * w : (i + 1) * w].bitcast(FP8X4),
+                    scales=ws[:, i * w : (i + 1) * w],
+                    in_=gw_t[key][:, 4 * i * w : 4 * (i + 1) * w],
+                )
+            wc_t[key] = (wc, ws)
 
         def mm(g, h):
             ec, es = ec_t[g]
-            wc, ws = wc_t[(g, h)]
+            wc, ws = wc_t[(g // 2, h)]
+            cols = slice((g % 2) * 512, (g % 2 + 1) * 512)
             for bt in range(2):
                 if (bt, h) not in acc:
                     acc[(bt, h)] = psum.tile(
@@ -263,8 +272,8 @@ def tile_lagrangenet_kernel(tc, x, min_x, max_x, W, dof, out):
                     out=acc[(bt, h)][:],
                     lhsT=ec[:, bt * P : (bt + 1) * P].bitcast(FP8X4),
                     lhsT_scale=es[:, bt * P : (bt + 1) * P],
-                    rhs=wc[:].bitcast(FP8X4),
-                    rhs_scale=ws[:],
+                    rhs=wc[:, cols].bitcast(FP8X4),
+                    rhs_scale=ws[:, cols],
                     start=(g == 0),
                     stop=(g == n_pass - 1),
                 )
@@ -309,8 +318,7 @@ def tile_lagrangenet_kernel(tc, x, min_x, max_x, W, dof, out):
             if last:
                 a2(s)
             if 1 <= s <= n_pass:
-                for g, h in items(s - 1):
-                    qw(g, h)
+                qw(((s - 1) // 2, (s - 1) % 2))
             if last:
                 qe(s)
             if s < n_pass and not last:

@@ -22,7 +22,7 @@ WR_BUFS = 24
 
 def dve_units(s):
     if s == 0:
-        return (0, 2)
+        return (3,)
     if s == 1:
         return (0, 1)
     if s == 31:
@@ -43,8 +43,8 @@ def tile_lagrangenet_kernel(tc, x, min_x, max_x, W, dof, out):
         ctx.enter_context(tc.manual_schedule())
         const = ctx.enter_context(tc.tile_pool(name="const", bufs=1))
         wrp = ctx.enter_context(tc.tile_pool(name="wrp", bufs=WR_BUFS))
-        gwp = ctx.enter_context(tc.tile_pool(name="gwp", bufs=3))
-        wcp = ctx.enter_context(tc.tile_pool(name="wcp", bufs=3))
+        gwp = ctx.enter_context(tc.tile_pool(name="gwp", bufs=6))
+        wcp = ctx.enter_context(tc.tile_pool(name="wcp", bufs=6))
         ap_ = ctx.enter_context(tc.tile_pool(name="ap", bufs=2))
         gep = ctx.enter_context(tc.tile_pool(name="gep", bufs=3))
         ecp = ctx.enter_context(tc.tile_pool(name="ecp", bufs=5))
@@ -228,10 +228,9 @@ def tile_lagrangenet_kernel(tc, x, min_x, max_x, W, dof, out):
         def unit(g, r):
             c, gl = pass_chunk[g]
             h = r // 2
-            key = (g // 2, h)
-            if key not in gw_t:
-                gw_t[key] = gwp.tile([P, 4 * N], BF16, name="gw", tag="gw", align_bytes=64)
-            gw32 = gw_t[key][:].bitcast(F32)[:, (g % 2) * N : (g % 2 + 1) * N]
+            if (g, h) not in gw_t:
+                gw_t[(g, h)] = gwp.tile([P, 2 * N], BF16, name="gw", tag="gw", align_bytes=64)
+            gw32 = gw_t[(g, h)][:].bitcast(F32)
             tw = psum.tile([P, 4, P], F32, name="tw", tag=next_bank())
             for jj in range(2):
                 j = 2 * r + jj
@@ -246,23 +245,15 @@ def tile_lagrangenet_kernel(tc, x, min_x, max_x, W, dof, out):
             try_load()
             return dst, src
 
-        def qw(key):
-            wc = wcp.tile([P, N], U32, name="wc", tag="wc", align_bytes=64)
-            ws = wcp.tile([P, N], U8, name="ws", tag="ws", align_bytes=64)
-            pieces = 2 if key == (n_pass // 2 - 1, 1) else 1
-            w = N // pieces
-            for i in range(pieces):
-                nc.vector.quantize_mx(
-                    out=wc[:, i * w : (i + 1) * w].bitcast(FP8X4),
-                    scales=ws[:, i * w : (i + 1) * w],
-                    in_=gw_t[key][:, 4 * i * w : 4 * (i + 1) * w],
-                )
-            wc_t[key] = (wc, ws)
+        def qw(g, h):
+            wc = wcp.tile([P, 512], U32, name="wc", tag="wc", align_bytes=64)
+            ws = wcp.tile([P, 512], U8, name="ws", tag="ws", align_bytes=64)
+            nc.vector.quantize_mx(out=wc[:].bitcast(FP8X4), scales=ws[:], in_=gw_t[(g, h)][:])
+            wc_t[(g, h)] = (wc, ws)
 
         def mm(g, h):
             ec, es = ec_t[g]
-            wc, ws = wc_t[(g // 2, h)]
-            cols = slice((g % 2) * 512, (g % 2 + 1) * 512)
+            wc, ws = wc_t[(g, h)]
             for bt in range(2):
                 if (bt, h) not in acc:
                     acc[(bt, h)] = psum.tile(
@@ -272,8 +263,8 @@ def tile_lagrangenet_kernel(tc, x, min_x, max_x, W, dof, out):
                     out=acc[(bt, h)][:],
                     lhsT=ec[:, bt * P : (bt + 1) * P].bitcast(FP8X4),
                     lhsT_scale=es[:, bt * P : (bt + 1) * P],
-                    rhs=wc[:, cols].bitcast(FP8X4),
-                    rhs_scale=ws[:, cols],
+                    rhs=wc[:].bitcast(FP8X4),
+                    rhs_scale=ws[:],
                     start=(g == 0),
                     stop=(g == n_pass - 1),
                 )
@@ -297,7 +288,7 @@ def tile_lagrangenet_kernel(tc, x, min_x, max_x, W, dof, out):
         for s in range(n_pass + 2):
             last = s == n_pass - 1
             late = []
-            if 1 <= s <= n_pass and not s == n_pass:
+            if 2 <= s < n_pass:
                 qe(s - 1)
             if s < n_pass:
                 on_dve = dve_units(s)
@@ -317,11 +308,16 @@ def tile_lagrangenet_kernel(tc, x, min_x, max_x, W, dof, out):
                     tx(s + 1, next_bank())
             if last:
                 a2(s)
+            if s == 1:
+                a2(0)
             if 1 <= s <= n_pass:
-                qw(((s - 1) // 2, (s - 1) % 2))
+                for g, h in items(s - 1):
+                    qw(g, h)
             if last:
                 qe(s)
-            if s < n_pass and not last:
+            if s == 1:
+                qe(0)
+            if 1 <= s < n_pass and not last:
                 a2(s)
             for dst, src in late:
                 leave(dst, src, True)

from contextlib import ExitStack

import concourse.mybir as mybir
from concourse.masks import make_identity

F32 = mybir.dt.float32
BF16 = mybir.dt.bfloat16
U32 = mybir.dt.uint32
U8 = mybir.dt.uint8
I32 = mybir.dt.int32
FP8X4 = mybir.dt.float8_e4m3fn_x4
ALU = mybir.AluOpType
ACTF = mybir.ActivationFunctionType

P = 128
K_PASS = 512
FLOPS = 2 * 256 * 1024 * 16384

CHUNKS = [1024] * 6 + [2048] * 5
WR_BUFS = 24


def dve_units(s):
    if s == 0:
        return (3,)
    if s == 1:
        return (0, 1)
    if s == 31:
        return ()
    return (3,)


def tile_lagrangenet_kernel(tc, x, min_x, max_x, W, dof, out):
    nc = tc.nc
    B, F = x.shape
    N, K = W.shape
    assert (B, F, N, K, dof) == (256, 256, 1024, 16384, 64)
    n_pass = K // K_PASS
    n_tiles = N // P
    steps = float(dof - 1)

    with ExitStack() as ctx:
        ctx.enter_context(tc.manual_schedule())
        const = ctx.enter_context(tc.tile_pool(name="const", bufs=1))
        wrp = ctx.enter_context(tc.tile_pool(name="wrp", bufs=WR_BUFS))
        gwp = ctx.enter_context(tc.tile_pool(name="gwp", bufs=6))
        wcp = ctx.enter_context(tc.tile_pool(name="wcp", bufs=6))
        ap_ = ctx.enter_context(tc.tile_pool(name="ap", bufs=2))
        gep = ctx.enter_context(tc.tile_pool(name="gep", bufs=3))
        ecp = ctx.enter_context(tc.tile_pool(name="ecp", bufs=5))
        resp = ctx.enter_context(tc.tile_pool(name="resp", bufs=4))
        psum = ctx.enter_context(tc.psum_pool(name="psum", bufs=1))

        x_sb = const.tile([P, 2, F], BF16, name="x_sb")
        nc.sync.dma_start(out=x_sb[:], in_=x.rearrange("(t p) f -> p t f", p=P))
        mn_bf = const.tile([P, 1], BF16, name="mn_bf")
        mx_bf = const.tile([P, 1], BF16, name="mx_bf")
        nc.scalar.dma_start(out=mn_bf[:], in_=min_x.partition_broadcast(P))
        nc.scalar.dma_start(out=mx_bf[:], in_=max_x.partition_broadcast(P))

        pass_chunk = []
        load_order = []
        chunk_start = []
        k0 = 0
        for c, kc in enumerate(CHUNKS):
            chunk_start.append(k0)
            k0 += kc
            for gl in range(kc // K_PASS):
                pass_chunk.append((c, gl))
            for j in range(n_tiles):
                load_order.append((c, j))
        assert k0 == K
        wr_tiles = {}
        wr_reads = {}
        loaded = [0]

        def try_load():
            while loaded[0] < len(load_order):
                n = loaded[0]
                if n >= WR_BUFS:
                    old = load_order[n - WR_BUFS]
                    if wr_reads.get(old, 0) < CHUNKS[old[0]] // K_PASS:
                        return
                c, j = load_order[n]
                kc = CHUNKS[c]
                wr = wrp.tile([P, kc], BF16, name="wr", tag="wr")
                nc.sync.dma_start(
                    out=wr[:], in_=W[j * P : (j + 1) * P, chunk_start[c] : chunk_start[c] + kc]
                )
                wr_tiles[(c, j)] = wr
                loaded[0] = n + 1

        try_load()

        ident = const.tile([P, P], F32, name="ident")
        make_identity(nc, ident[:])
        vi = const.tile([P, 2], I32, name="vi")
        nc.gpsimd.iota(vi[:], pattern=[[1, 2]], base=0, channel_multiplier=2)
        big = const.tile([P, P, 32], BF16, name="big")
        for lo, hi in ((0, 32), (32, P)):
            nc.gpsimd.tensor_scalar(
                out=big[:, lo:hi, :],
                in0=ident[:, lo:hi].unsqueeze(2).to_broadcast([P, hi - lo, 32]),
                scalar1=1.0,
                scalar2=0.0,
                op0=ALU.mult,
                op1=ALU.add,
            )
        bigf = big[:].rearrange("p f r -> p (f r)")

        warm_in = const.tile([P, 1], F32, name="warm_in")
        warm_out = const.tile([P, 1], F32, name="warm_out")
        nc.vector.memset(warm_in[:], 0.0)
        nc.scalar.activation(out=warm_out[:], in_=warm_in[:], func=ACTF.Abs)
        xf = const.tile([P, 2, F], F32, name="xf")
        nc.scalar.copy(out=xf[:], in_=x_sb[:])

        xtp = psum.tile([P, 2, B], F32, name="xtp", tag="acc11")
        for ft in range(2):
            for t in range(2):
                nc.tensor.transpose(
                    xtp[:, ft, t * P : (t + 1) * P], xf[:, t, ft * P : (ft + 1) * P], ident[:]
                )

        sc = const.tile([P, 8], F32, name="sc")
        mn = sc[:, 0:1]
        mx = sc[:, 1:2]
        nrg = sc[:, 2:3]
        nmn = sc[:, 3:4]
        c63 = sc[:, 4:5]
        k2 = sc[:, 5:6]
        nc.vector.tensor_copy(out=mn, in_=mn_bf[:])
        nc.vector.tensor_copy(out=mx, in_=mx_bf[:])
        nc.vector.tensor_sub(out=nrg, in0=mn, in1=mx)
        nc.vector.tensor_scalar(out=k2, in0=nrg, scalar1=-2.0, scalar2=None, op0=ALU.mult)
        nc.vector.tensor_scalar(out=nmn, in0=mn, scalar1=-1.0, scalar2=None, op0=ALU.mult)
        nc.vector.tensor_scalar(out=c63, in0=mn, scalar1=-steps, scalar2=None, op0=ALU.mult)
        vm = const.tile([P, 2], I32, name="vm")
        nc.vector.tensor_single_scalar(out=vm[:], in_=vi[:], scalar=dof - 1, op=ALU.bitwise_and)
        vf = const.tile([P, 2], F32, name="vf")
        nc.vector.tensor_copy(out=vf[:], in_=vm[:])
        bias = const.tile([P, 2], F32, name="bias")
        nc.vector.tensor_scalar(out=bias[:], in0=vf[:], scalar1=nrg, scalar2=c63, op0=ALU.mult, op1=ALU.add)

        xT = const.tile([P, 2, B], BF16, name="xT")
        below = const.tile([P, 2, B], F32, name="below")
        side = const.tile([P, 2, B], F32, name="side")

        def push_out(ft):
            nc.vector.tensor_scalar(
                out=below[:, ft, :], in0=xtp[:, ft, :], scalar1=mn, scalar2=None, op0=ALU.is_lt
            )
            nc.vector.scalar_tensor_tensor(
                out=side[:, ft, :], in0=xtp[:, ft, :], scalar=mx, in1=below[:, ft, :],
                op0=ALU.is_gt, op1=ALU.subtract,
            )
            nc.vector.scalar_tensor_tensor(
                out=xT[:, ft, :], in0=side[:, ft, :], scalar=k2, in1=xtp[:, ft, :],
                op0=ALU.mult, op1=ALU.add,
            )

        push_out(0)

        bank_use = [0]

        def next_bank():
            tag = "rot%d" % (bank_use[0] % 4)
            bank_use[0] += 1
            return tag

        acc = {}
        xb_t = {}
        a_t = {}
        ge_t = {}
        ec_t = {}
        gw_t = {}
        wc_t = {}

        def tx(g, tag):
            xb = psum.tile([P, 2, B], F32, name="xb", tag=tag)
            for u in range(2):
                m = 2 * (g % 16) + u
                nc.tensor.matmul(
                    xb[:, u, :],
                    lhsT=bigf[:, m * P : (m + 1) * P],
                    rhs=xT[:, g // 16, :],
                    start=True,
                    stop=True,
                )
            xb_t[g] = xb

        def a1(g):
            a = ap_.tile([P, 2, 2 * B], F32, name="a", tag="a")
            for e in range(2):
                nc.scalar.activation(
                    out=a[:, e, :].rearrange("p (b u) -> p b u", u=2),
                    in_=xb_t[g][:].rearrange("p u b -> p b u"),
                    func=ACTF.Abs,
                    bias=bias[:, e : e + 1],
                    scale=steps,
                )
            a_t[g] = a

        def a2(g):
            ge = gep.tile([P, 4 * B], BF16, name="ge", tag="ge", align_bytes=64)
            nc.vector.tensor_scalar(
                out=ge[:].rearrange("p (c e) -> p c e", e=2),
                in0=a_t[g][:].rearrange("p e c -> p c e"),
                scalar1=mx,
                scalar2=nmn,
                op0=ALU.subtract,
                op1=ALU.min,
            )
            ge_t[g] = ge

        def qe(g):
            ec = ecp.tile([P, B], U32, name="ec", tag="ec", align_bytes=64)
            es = ecp.tile([P, B], U8, name="es", tag="es", align_bytes=64)
            nc.vector.quantize_mx(out=ec[:].bitcast(FP8X4), scales=es[:], in_=ge_t[g][:])
            ec_t[g] = (ec, es)

        def leave(dst, src, on_dve):
            if on_dve:
                nc.vector.tensor_copy(out=dst, in_=src)
            else:
                nc.scalar.copy(out=dst, in_=src)

        def unit(g, r):
            c, gl = pass_chunk[g]
            h = r // 2
            if (g, h) not in gw_t:
                gw_t[(g, h)] = gwp.tile([P, 2 * N], BF16, name="gw", tag="gw", align_bytes=64)
            gw32 = gw_t[(g, h)][:].bitcast(F32)
            tw = psum.tile([P, 4, P], F32, name="tw", tag=next_bank())
            for jj in range(2):
                j = 2 * r + jj
                w32 = wr_tiles[(c, j)][:].bitcast(F32)
                for u in range(2):
                    w0 = 256 * gl + P * u
                    nc.tensor.transpose(tw[:, 2 * jj + u, :], w32[:, w0 : w0 + P], ident[:])
                wr_reads[(c, j)] = wr_reads.get((c, j), 0) + 1
            part = r % 2
            dst = gw32[:, 512 * part : 512 * (part + 1)].rearrange("p (j n u) -> p j n u", j=2, u=2)
            src = tw[:].rearrange("p (j u) n -> p j n u", u=2)
            try_load()
            return dst, src

        def qw(g, h):
            wc = wcp.tile([P, 512], U32, name="wc", tag="wc", align_bytes=64)
            ws = wcp.tile([P, 512], U8, name="ws", tag="ws", align_bytes=64)
            nc.vector.quantize_mx(out=wc[:].bitcast(FP8X4), scales=ws[:], in_=gw_t[(g, h)][:])
            wc_t[(g, h)] = (wc, ws)

        def mm(g, h):
            ec, es = ec_t[g]
            wc, ws = wc_t[(g, h)]
            for bt in range(2):
                if (bt, h) not in acc:
                    acc[(bt, h)] = psum.tile(
                        [P, 512], F32, name="acc%d%d" % (bt, h), tag="acc%d%d" % (bt, h)
                    )
                nc.tensor.matmul_mx(
                    out=acc[(bt, h)][:],
                    lhsT=ec[:, bt * P : (bt + 1) * P].bitcast(FP8X4),
                    lhsT_scale=es[:, bt * P : (bt + 1) * P],
                    rhs=wc[:].bitcast(FP8X4),
                    rhs_scale=ws[:],
                    start=(g == 0),
                    stop=(g == n_pass - 1),
                )

        def finish(h):
            for bt in range(2):
                res = resp.tile([P, 512], F32, name="res", tag="res")
                if bt == 0:
                    nc.scalar.mul(out=res[:], in_=acc[(bt, h)][:], mul=-1.0)
                else:
                    nc.vector.tensor_scalar(
                        out=res[:], in0=acc[(bt, h)][:], scalar1=-1.0, scalar2=None, op0=ALU.mult
                    )
                nc.sync.dma_start(
                    out=out[bt * P : (bt + 1) * P, h * 512 : (h + 1) * 512], in_=res[:]
                )

        def items(s):
            return ((2 * (s // 2), s % 2), (2 * (s // 2) + 1, s % 2))

        for s in range(n_pass + 2):
            last = s == n_pass - 1
            late = []
            if 2 <= s < n_pass:
                qe(s - 1)
            if s < n_pass:
                on_dve = dve_units(s)
                (ga, h), (gb, hb) = items(s)
                order = ((ga, 2 * h), (gb, 2 * h), (ga, 2 * h + 1), (gb, 2 * h + 1))
                for i, (g, r) in enumerate(order):
                    dst, src = unit(g, r)
                    if s >= 2 and i in on_dve:
                        late.append((dst, src))
                    else:
                        leave(dst, src, i in on_dve)
                if s == 0:
                    tx(0, "acc10")
                    tx(1, "acc01")
                    a1(0)
                elif s + 1 < n_pass:
                    tx(s + 1, next_bank())
            if last:
                a2(s)
            if s == 1:
                a2(0)
            if 1 <= s <= n_pass:
                for g, h in items(s - 1):
                    qw(g, h)
            if last:
                qe(s)
            if s == 1:
                qe(0)
            if 1 <= s < n_pass and not last:
                a2(s)
            for dst, src in late:
                leave(dst, src, True)
            if s == 1:
                push_out(1)
            if s + 1 < n_pass:
                a1(s + 1)
            if s >= 2:
                for g, h in items(s - 2):
                    mm(g, h)
                    if g == n_pass - 1:
                        finish(h)
